import numpy as np
import ml_dtypes

BF16 = ml_dtypes.bfloat16


def bf(x):
    return np.asarray(x, np.float32).astype(BF16)


def f32(x):
    return np.asarray(x, np.float32)


def f64(x):
    return np.asarray(x).astype(np.float64)


def striped(idx):
    return np.tile(idx.reshape(-1, 16).T, (8, 1))


S, D, O, K, N = 1024, 128, 128, 4, 512
TEMP = 0.07
EPS = 1e-12


def l2norm_rows(v):
    return v / np.maximum(np.sqrt(np.sum(v * v, axis=-1, keepdims=True)), EPS)


def setup_inputs():
    return {"table": bf(np.random.standard_normal((S, D))), "w": bf(np.random.standard_normal((D, O))), "offs": striped(np.random.permutation(S)[:N])}


def reference(table, w, offs):
    idx = offs[:16].T.reshape(-1)
    mn = l2norm_rows(f64(table))
    pn = l2norm_rows(f64(w).T)
    return pn @ mn[idx].T / TEMP

@@ -1,0 +1,65 @@
+import concourse.mybir as mybir
+from concourse.masks import make_identity
+
+P = 128
+SLOTS = 1024
+PICKED = 512
+BLOCKS = SLOTS // P
+HALF = SLOTS // 2
+TEMPERATURE = 0.07
+EPS = 1e-12
+FLOPS = 2 * P * P * PICKED
+
+BF16, F32, U16 = mybir.dt.bfloat16, mybir.dt.float32, mybir.dt.uint16
+SQUARE = mybir.ActivationFunctionType.Square
+SQRT = mybir.ActivationFunctionType.Sqrt
+MULT = mybir.AluOpType.mult
+
+
+def tile_memcontrastiveloss_kernel(tc, table, w, offs, out):
+    nc = tc.nc
+    with (
+        tc.tile_pool(name="held", bufs=1) as held,
+        tc.psum_pool(name="psum", bufs=1) as psum,
+    ):
+        offsets = held.tile([P, PICKED // 16], U16, name="offsets")
+        nc.sync.dma_start(offsets[:], offs)
+        rows = held.tile([P, BLOCKS, P], BF16, name="rows")
+        nc.sync.dma_start(rows[:], table.rearrange("(b p) d -> p b d", p=P))
+        weights = held.tile([P, P], BF16, name="weights")
+        nc.scalar.dma_start(weights[:], w)
+        identity = held.tile([P, P], BF16, name="identity")
+        make_identity(nc, identity[:])
+
+        sumsq = held.tile([P, BLOCKS + 1], F32, name="sumsq")
+        squares = held.tile([P, P], F32, name="squares")
+        for b in range(BLOCKS):
+            nc.scalar.activation(squares[:], rows[:, b, :], SQUARE, accum_out=sumsq[:, b : b + 1])
+        flipped_w = psum.tile([P, P], BF16, name="flipped_w")
+        nc.tensor.transpose(flipped_w[:], weights[:], identity[:])
+        nc.scalar.activation(squares[:], flipped_w[:], SQUARE, accum_out=sumsq[:, BLOCKS : BLOCKS + 1])
+
+        norm = held.tile([P, BLOCKS + 1], F32, name="norm")
+        inverse = held.tile([P, BLOCKS + 1], F32, name="inverse")
+        nc.vector.tensor_scalar_max(sumsq[:], sumsq[:], EPS * EPS)
+        nc.scalar.activation(norm[:], sumsq[:], SQRT)
+        nc.vector.reciprocal(inverse[:], norm[:])
+
+        normed = held.tile([P, BLOCKS, P], BF16, name="normed")
+        window = held.tile([P, SLOTS], BF16, name="window")
+        for h in range(2):
+            flipped = psum.tile([P, HALF], BF16, name=f"flipped{h}")
+            for k in range(BLOCKS // 2):
+                b = h * (BLOCKS // 2) + k
+                nc.vector.tensor_scalar_mul(normed[:, b, :], rows[:, b, :], inverse[:, b : b + 1])
+                nc.tensor.transpose(flipped[:, k * P : (k + 1) * P], normed[:, b, :], identity[:])
+            nc.vector.tensor_copy(window[:, h * HALF : (h + 1) * HALF], flipped[:])
+
+        logits = psum.tile([P, PICKED], F32, name="logits")
+        nc.tensor.matmul(logits[:], weights[:], window[:].indirect(offsets[:]), start=True, stop=True)
+
+        scaled = held.tile([P, PICKED], F32, name="scaled")
+        nc.vector.tensor_scalar(
+            scaled[:], logits[:], inverse[:, BLOCKS : BLOCKS + 1], 1.0 / TEMPERATURE, MULT, MULT
+        )
+        nc.sync.dma_start(out, scaled[:])

@@ -31,6 +31,10 @@ def tile_memcontrastiveloss_kernel(tc, table, w, offs, out):
         identity = held.tile([P, P], BF16, name="identity")
         make_identity(nc, identity[:])
 
+        scratch = held.tile([P, 1], F32, name="scratch")
+        nc.vector.memset(scratch[:], 1.0)
+        nc.scalar.activation(scratch[:], scratch[:], SQRT)
+
         sumsq = held.tile([P, BLOCKS + 1], F32, name="sumsq")
         squares = held.tile([P, P], F32, name="squares")
         for b in range(BLOCKS):

@@ -4,8 +4,9 @@ from concourse.masks import make_identity
 P = 128
 SLOTS = 1024
 PICKED = 512
-BLOCKS = SLOTS // P
+CHUNKS = SLOTS // (2 * P)
 HALF = SLOTS // 2
+PAD = 8
 TEMPERATURE = 0.07
 EPS = 1e-12
 FLOPS = 2 * P * P * PICKED
@@ -22,10 +23,15 @@ def tile_memcontrastiveloss_kernel(tc, table, w, offs, out):
         tc.tile_pool(name="held", bufs=1) as held,
         tc.psum_pool(name="psum", bufs=1) as psum,
     ):
+        rows = []
+        for c in range(CHUNKS):
+            chunk = held.tile([P, 2, P], BF16, name=f"rows{c}")
+            nc.sync.dma_start(
+                chunk[:], table[c * 2 * P : (c + 1) * 2 * P, :].rearrange("(e p) d -> p e d", p=P)
+            )
+            rows.append(chunk)
         offsets = held.tile([P, PICKED // 16], U16, name="offsets")
         nc.sync.dma_start(offsets[:], offs)
-        rows = held.tile([P, BLOCKS, P], BF16, name="rows")
-        nc.sync.dma_start(rows[:], table.rearrange("(b p) d -> p b d", p=P))
         weights = held.tile([P, P], BF16, name="weights")
         nc.scalar.dma_start(weights[:], w)
         identity = held.tile([P, P], BF16, name="identity")
@@ -35,35 +41,46 @@ def tile_memcontrastiveloss_kernel(tc, table, w, offs, out):
         nc.vector.memset(scratch[:], 1.0)
         nc.scalar.activation(scratch[:], scratch[:], SQRT)
 
-        sumsq = held.tile([P, BLOCKS + 1], F32, name="sumsq")
-        squares = held.tile([P, P], F32, name="squares")
-        for b in range(BLOCKS):
-            nc.scalar.activation(squares[:], rows[:, b, :], SQUARE, accum_out=sumsq[:, b : b + 1])
-        flipped_w = psum.tile([P, P], BF16, name="flipped_w")
-        nc.tensor.transpose(flipped_w[:], weights[:], identity[:])
-        nc.scalar.activation(squares[:], flipped_w[:], SQUARE, accum_out=sumsq[:, BLOCKS : BLOCKS + 1])
+        sumsq = held.tile([P, 2, PAD], F32, name="sumsq")
+        squares_s = held.tile([P, P], F32, name="squares_s")
+        squares_v = held.tile([P, P], F32, name="squares_v")
+        for c in range(CHUNKS):
+            nc.scalar.activation(squares_s[:], rows[c][:, 0, :], SQUARE, accum_out=sumsq[:, 0, c : c + 1])
+            nc.vector.scalar_tensor_tensor(
+                squares_v[:], rows[c][:, 1, :], 1.0, rows[c][:, 1, :], MULT, MULT,
+                accum_out=sumsq[:, 1, c : c + 1],
+            )
 
-        norm = held.tile([P, BLOCKS + 1], F32, name="norm")
-        inverse = held.tile([P, BLOCKS + 1], F32, name="inverse")
-        nc.vector.tensor_scalar_max(sumsq[:], sumsq[:], EPS * EPS)
-        nc.scalar.activation(norm[:], sumsq[:], SQRT)
+        floored = held.tile([P, 2, CHUNKS], F32, name="floored")
+        norm = held.tile([P, 2, CHUNKS], F32, name="norm")
+        inverse = held.tile([P, 2, CHUNKS], F32, name="inverse")
+        nc.vector.tensor_scalar_max(floored[:], sumsq[:, :, 0:CHUNKS], EPS * EPS)
+        nc.scalar.activation(norm[:], floored[:], SQRT)
         nc.vector.reciprocal(inverse[:], norm[:])
 
-        normed = held.tile([P, BLOCKS, P], BF16, name="normed")
         window = held.tile([P, SLOTS], BF16, name="window")
         for h in range(2):
             flipped = psum.tile([P, HALF], BF16, name=f"flipped{h}")
-            for k in range(BLOCKS // 2):
-                b = h * (BLOCKS // 2) + k
-                nc.vector.tensor_scalar_mul(normed[:, b, :], rows[:, b, :], inverse[:, b : b + 1])
-                nc.tensor.transpose(flipped[:, k * P : (k + 1) * P], normed[:, b, :], identity[:])
+            for k in range(HALF // P):
+                c, e = (h * HALF + k * P) // (2 * P), k % 2
+                normed = held.tile([P, P], BF16, name=f"normed{c}{e}")
+                nc.vector.tensor_scalar_mul(normed[:], rows[c][:, e, :], inverse[:, e, c : c + 1])
+                nc.tensor.transpose(flipped[:, k * P : (k + 1) * P], normed[:], identity[:])
             nc.vector.tensor_copy(window[:, h * HALF : (h + 1) * HALF], flipped[:])
+
+        flipped_w = psum.tile([P, P], BF16, name="flipped_w")
+        w_sumsq = held.tile([P, 1], F32, name="w_sumsq")
+        w_norm = held.tile([P, 1], F32, name="w_norm")
+        w_scale = held.tile([P, 1], F32, name="w_scale")
+        nc.tensor.transpose(flipped_w[:], weights[:], identity[:])
+        nc.scalar.activation(squares_s[:], flipped_w[:], SQUARE, accum_out=w_sumsq[:])
+        nc.vector.tensor_scalar_max(w_sumsq[:], w_sumsq[:], EPS * EPS)
+        nc.scalar.activation(w_norm[:], w_sumsq[:], SQRT, scale=TEMPERATURE * TEMPERATURE)
+        nc.vector.reciprocal(w_scale[:], w_norm[:])
 
         logits = psum.tile([P, PICKED], F32, name="logits")
         nc.tensor.matmul(logits[:], weights[:], window[:].indirect(offsets[:]), start=True, stop=True)
 
         scaled = held.tile([P, PICKED], F32, name="scaled")
-        nc.vector.tensor_scalar(
-            scaled[:], logits[:], inverse[:, BLOCKS : BLOCKS + 1], 1.0 / TEMPERATURE, MULT, MULT
-        )
+        nc.vector.tensor_scalar_mul(scaled[:], logits[:], w_scale[:])
         nc.sync.dma_start(out, scaled[:])

@@ -4,8 +4,8 @@ from concourse.masks import make_identity
 P = 128
 SLOTS = 1024
 PICKED = 512
-CHUNKS = SLOTS // (2 * P)
-HALF = SLOTS // 2
+CHUNK = 2 * P
+CHUNKS = SLOTS // CHUNK
 PAD = 8
 TEMPERATURE = 0.07
 EPS = 1e-12
@@ -27,7 +27,7 @@ def tile_memcontrastiveloss_kernel(tc, table, w, offs, out):
         for c in range(CHUNKS):
             chunk = held.tile([P, 2, P], BF16, name=f"rows{c}")
             nc.sync.dma_start(
-                chunk[:], table[c * 2 * P : (c + 1) * 2 * P, :].rearrange("(e p) d -> p e d", p=P)
+                chunk[:], table[c * CHUNK : (c + 1) * CHUNK, :].rearrange("(e p) d -> p e d", p=P)
             )
             rows.append(chunk)
         offsets = held.tile([P, PICKED // 16], U16, name="offsets")
@@ -41,32 +41,34 @@ def tile_memcontrastiveloss_kernel(tc, table, w, offs, out):
         nc.vector.memset(scratch[:], 1.0)
         nc.scalar.activation(scratch[:], scratch[:], SQRT)
 
-        sumsq = held.tile([P, 2, PAD], F32, name="sumsq")
         squares_s = held.tile([P, P], F32, name="squares_s")
         squares_v = held.tile([P, P], F32, name="squares_v")
+        window = held.tile([P, SLOTS], BF16, name="window")
+
         for c in range(CHUNKS):
-            nc.scalar.activation(squares_s[:], rows[c][:, 0, :], SQUARE, accum_out=sumsq[:, 0, c : c + 1])
+            sumsq = held.tile([P, 2, PAD], F32, name=f"sumsq{c}")
+            nc.scalar.activation(squares_s[:], rows[c][:, 0, :], SQUARE, accum_out=sumsq[:, 0, 0:1])
             nc.vector.scalar_tensor_tensor(
                 squares_v[:], rows[c][:, 1, :], 1.0, rows[c][:, 1, :], MULT, MULT,
-                accum_out=sumsq[:, 1, c : c + 1],
+                accum_out=sumsq[:, 1, 0:1],
             )
 
-        floored = held.tile([P, 2, CHUNKS], F32, name="floored")
-        norm = held.tile([P, 2, CHUNKS], F32, name="norm")
-        inverse = held.tile([P, 2, CHUNKS], F32, name="inverse")
-        nc.vector.tensor_scalar_max(floored[:], sumsq[:, :, 0:CHUNKS], EPS * EPS)
-        nc.scalar.activation(norm[:], floored[:], SQRT)
-        nc.vector.reciprocal(inverse[:], norm[:])
+            floored = held.tile([P, 2, 1], F32, name=f"floored{c}")
+            norm = held.tile([P, 2, 1], F32, name=f"norm{c}")
+            inverse = held.tile([P, 2, 1], F32, name=f"inverse{c}")
+            nc.vector.tensor_scalar_max(floored[:], sumsq[:, :, 0:1], EPS * EPS)
+            nc.scalar.activation(norm[:], floored[:], SQRT)
+            nc.vector.reciprocal(inverse[:], norm[:])
 
-        window = held.tile([P, SLOTS], BF16, name="window")
-        for h in range(2):
-            flipped = psum.tile([P, HALF], BF16, name=f"flipped{h}")
-            for k in range(HALF // P):
-                c, e = (h * HALF + k * P) // (2 * P), k % 2
-                normed = held.tile([P, P], BF16, name=f"normed{c}{e}")
-                nc.vector.tensor_scalar_mul(normed[:], rows[c][:, e, :], inverse[:, e, c : c + 1])
-                nc.tensor.transpose(flipped[:, k * P : (k + 1) * P], normed[:], identity[:])
-            nc.vector.tensor_copy(window[:, h * HALF : (h + 1) * HALF], flipped[:])
+            normed = held.tile([P, 2, P], BF16, name=f"normed{c}")
+            flipped = psum.tile([P, CHUNK], BF16, name=f"flipped{c}")
+            for e in range(2):
+                nc.vector.tensor_scalar_mul(normed[:, e, :], rows[c][:, e, :], inverse[:, e, :])
+                nc.tensor.transpose(flipped[:, e * P : (e + 1) * P], normed[:, e, :], identity[:])
+            if c % 2 == 0:
+                nc.scalar.copy(window[:, c * CHUNK : (c + 1) * CHUNK], flipped[:])
+            else:
+                nc.vector.tensor_copy(window[:, c * CHUNK : (c + 1) * CHUNK], flipped[:])
 
         flipped_w = psum.tile([P, P], BF16, name="flipped_w")
         w_sumsq = held.tile([P, 1], F32, name="w_sumsq")

@@ -6,6 +6,7 @@ SLOTS = 1024
 PICKED = 512
 CHUNK = 2 * P
 CHUNKS = SLOTS // CHUNK
+PIECE = PICKED // 2
 PAD = 8
 TEMPERATURE = 0.07
 EPS = 1e-12
@@ -13,9 +14,9 @@ FLOPS = 2 * P * P * PICKED
 
 BF16, F32, U16 = mybir.dt.bfloat16, mybir.dt.float32, mybir.dt.uint16
 SQUARE = mybir.ActivationFunctionType.Square
-SQRT = mybir.ActivationFunctionType.Sqrt
-MULT = mybir.AluOpType.mult
-
+RSQRT = mybir.ActivationFunctionType.Abs_reciprocal_sqrt
+COPY = mybir.ActivationFunctionType.Copy
+MULT, MIN = mybir.AluOpType.mult, mybir.AluOpType.min
 
 def tile_memcontrastiveloss_kernel(tc, table, w, offs, out):
     nc = tc.nc
@@ -26,20 +27,21 @@ def tile_memcontrastiveloss_kernel(tc, table, w, offs, out):
         rows = []
         for c in range(CHUNKS):
             chunk = held.tile([P, 2, P], BF16, name=f"rows{c}")
-            nc.sync.dma_start(
-                chunk[:], table[c * CHUNK : (c + 1) * CHUNK, :].rearrange("(e p) d -> p e d", p=P)
+            queue = nc.sync if c % 2 == 0 else nc.scalar
+            queue.dma_start(
+                chunk[:], table[c * CHUNK : (c + 1) * CHUNK, :].rearrange("(p e) d -> p e d", e=2)
             )
             rows.append(chunk)
         offsets = held.tile([P, PICKED // 16], U16, name="offsets")
         nc.sync.dma_start(offsets[:], offs)
         weights = held.tile([P, P], BF16, name="weights")
-        nc.scalar.dma_start(weights[:], w)
+        nc.sync.dma_start(weights[:], w)
         identity = held.tile([P, P], BF16, name="identity")
         make_identity(nc, identity[:])
 
         scratch = held.tile([P, 1], F32, name="scratch")
         nc.vector.memset(scratch[:], 1.0)
-        nc.scalar.activation(scratch[:], scratch[:], SQRT)
+        nc.scalar.activation(scratch[:], scratch[:], RSQRT)
 
         squares_s = held.tile([P, P], F32, name="squares_s")
         squares_v = held.tile([P, P], F32, name="squares_v")
@@ -52,37 +54,41 @@ def tile_memcontrastiveloss_kernel(tc, table, w, offs, out):
                 squares_v[:], rows[c][:, 1, :], 1.0, rows[c][:, 1, :], MULT, MULT,
                 accum_out=sumsq[:, 1, 0:1],
             )
-
-            floored = held.tile([P, 2, 1], F32, name=f"floored{c}")
-            norm = held.tile([P, 2, 1], F32, name=f"norm{c}")
             inverse = held.tile([P, 2, 1], F32, name=f"inverse{c}")
-            nc.vector.tensor_scalar_max(floored[:], sumsq[:, :, 0:1], EPS * EPS)
-            nc.scalar.activation(norm[:], floored[:], SQRT)
-            nc.vector.reciprocal(inverse[:], norm[:])
+            nc.scalar.activation(inverse[:], sumsq[:, :, 0:1], RSQRT)
 
             normed = held.tile([P, 2, P], BF16, name=f"normed{c}")
             flipped = psum.tile([P, CHUNK], BF16, name=f"flipped{c}")
             for e in range(2):
-                nc.vector.tensor_scalar_mul(normed[:, e, :], rows[c][:, e, :], inverse[:, e, :])
+                nc.vector.scalar_tensor_tensor(
+                    normed[:, e, :], inverse[:, e, :].to_broadcast([P, P]), 1.0 / EPS,
+                    rows[c][:, e, :], MIN, MULT,
+                )
                 nc.tensor.transpose(flipped[:, e * P : (e + 1) * P], normed[:, e, :], identity[:])
+            in_slot_order = flipped[:].rearrange("d (e p) -> d p e", e=2)
+            columns = window[:, c * CHUNK : (c + 1) * CHUNK].rearrange("d (p e) -> d p e", e=2)
             if c % 2 == 0:
-                nc.scalar.copy(window[:, c * CHUNK : (c + 1) * CHUNK], flipped[:])
+                nc.scalar.copy(columns, in_slot_order)
             else:
-                nc.vector.tensor_copy(window[:, c * CHUNK : (c + 1) * CHUNK], flipped[:])
+                nc.vector.tensor_copy(columns, in_slot_order)
 
         flipped_w = psum.tile([P, P], BF16, name="flipped_w")
         w_sumsq = held.tile([P, 1], F32, name="w_sumsq")
-        w_norm = held.tile([P, 1], F32, name="w_norm")
+        w_inverse = held.tile([P, 1], F32, name="w_inverse")
         w_scale = held.tile([P, 1], F32, name="w_scale")
         nc.tensor.transpose(flipped_w[:], weights[:], identity[:])
         nc.scalar.activation(squares_s[:], flipped_w[:], SQUARE, accum_out=w_sumsq[:])
-        nc.vector.tensor_scalar_max(w_sumsq[:], w_sumsq[:], EPS * EPS)
-        nc.scalar.activation(w_norm[:], w_sumsq[:], SQRT, scale=TEMPERATURE * TEMPERATURE)
-        nc.vector.reciprocal(w_scale[:], w_norm[:])
+        nc.scalar.activation(w_inverse[:], w_sumsq[:], RSQRT, scale=TEMPERATURE * TEMPERATURE)
+        nc.vector.tensor_scalar_min(w_scale[:], w_inverse[:], 1.0 / (TEMPERATURE * EPS))
 
-        logits = psum.tile([P, PICKED], F32, name="logits")
-        nc.tensor.matmul(logits[:], weights[:], window[:].indirect(offsets[:]), start=True, stop=True)
-
-        scaled = held.tile([P, PICKED], F32, name="scaled")
-        nc.vector.tensor_scalar_mul(scaled[:], logits[:], w_scale[:])
-        nc.sync.dma_start(out, scaled[:])
+        for j in range(2):
+            logits = psum.tile([P, PIECE], F32, name=f"logits{j}")
+            scaled = held.tile([P, PIECE], F32, name=f"scaled{j}")
+            piece = offsets[:, j * (PIECE // 16) : (j + 1) * (PIECE // 16)]
+            nc.tensor.matmul(logits[:], weights[:], window[:].indirect(piece), start=True, stop=True)
+            if j == 0:
+                nc.vector.tensor_scalar_mul(scaled[:], logits[:], w_scale[:])
+                nc.sync.dma_start(out[:, j * PIECE : (j + 1) * PIECE], scaled[:])
+            else:
+                nc.scalar.activation(scaled[:], logits[:], COPY, scale=w_scale[:])
+                nc.scalar.dma_start(out[:, j * PIECE : (j + 1) * PIECE], scaled[:])

@@ -38,51 +38,61 @@ def tile_memcontrastiveloss_kernel(tc, table, w, offs, out):
         nc.sync.dma_start(weights[:], w)
         identity = held.tile([P, P], BF16, name="identity")
         make_identity(nc, identity[:])
+        identity_f32 = held.tile([P, P], F32, name="identity_f32")
+        make_identity(nc, identity_f32[:])
 
         scratch = held.tile([P, 1], F32, name="scratch")
         nc.vector.memset(scratch[:], 1.0)
         nc.scalar.activation(scratch[:], scratch[:], RSQRT)
 
-        squares_s = held.tile([P, P], F32, name="squares_s")
-        squares_v = held.tile([P, P], F32, name="squares_v")
         window = held.tile([P, SLOTS], BF16, name="window")
 
+        flipped, sumsq = [], []
         for c in range(CHUNKS):
-            sumsq = held.tile([P, 2, PAD], F32, name=f"sumsq{c}")
-            nc.scalar.activation(squares_s[:], rows[c][:, 0, :], SQUARE, accum_out=sumsq[:, 0, 0:1])
-            nc.vector.scalar_tensor_tensor(
-                squares_v[:], rows[c][:, 1, :], 1.0, rows[c][:, 1, :], MULT, MULT,
-                accum_out=sumsq[:, 1, 0:1],
-            )
-            inverse = held.tile([P, 2, 1], F32, name=f"inverse{c}")
-            nc.scalar.activation(inverse[:], sumsq[:, :, 0:1], RSQRT)
-
-            normed = held.tile([P, 2, P], BF16, name=f"normed{c}")
-            flipped = psum.tile([P, CHUNK], BF16, name=f"flipped{c}")
+            flipped.append(psum.tile([P, CHUNK], BF16, name=f"flipped{c}"))
             for e in range(2):
-                nc.vector.scalar_tensor_tensor(
-                    normed[:, e, :], inverse[:, e, :].to_broadcast([P, P]), 1.0 / EPS,
-                    rows[c][:, e, :], MIN, MULT,
+                nc.tensor.transpose(
+                    flipped[c][:, e * P : (e + 1) * P], rows[c][:, e, :], identity[:]
                 )
-                nc.tensor.transpose(flipped[:, e * P : (e + 1) * P], normed[:, e, :], identity[:])
-            in_slot_order = flipped[:].rearrange("d (e p) -> d p e", e=2)
-            columns = window[:, c * CHUNK : (c + 1) * CHUNK].rearrange("d (p e) -> d p e", e=2)
-            if c % 2 == 0:
-                nc.scalar.copy(columns, in_slot_order)
-            else:
-                nc.vector.tensor_copy(columns, in_slot_order)
+            sumsq.append(held.tile([P, 2, PAD], F32, name=f"sumsq{c}"))
+            squares = held.tile([P, 2, P], F32, name=f"squares{c}")
+            nc.scalar.activation(
+                squares[:, 0, :], rows[c][:, 0, :], SQUARE, accum_out=sumsq[c][:, 0, 0:1]
+            )
+            nc.vector.scalar_tensor_tensor(
+                squares[:, 1, :], rows[c][:, 1, :], 1.0, rows[c][:, 1, :], MULT, MULT,
+                accum_out=sumsq[c][:, 1, 0:1],
+            )
 
-        flipped_w = psum.tile([P, P], BF16, name="flipped_w")
+        for c in range(CHUNKS):
+            inverse = held.tile([P, 2, 1], F32, name=f"inverse{c}")
+            nc.scalar.activation(inverse[:], sumsq[c][:, :, 0:1], RSQRT)
+            spread = psum.tile([P, CHUNK], F32, name=f"spread{c}")
+            for e in range(2):
+                nc.tensor.transpose(
+                    spread[:, e * P : (e + 1) * P], inverse[:, e, :].to_broadcast([P, P]),
+                    identity_f32[:],
+                )
+            raw = held.tile([P, CHUNK], BF16, name=f"raw{c}")
+            nc.scalar.copy(raw[:], flipped[c][:])
+            nc.vector.scalar_tensor_tensor(
+                window[:, c * CHUNK : (c + 1) * CHUNK].rearrange("d (p e) -> d p e", e=2),
+                spread[:].rearrange("d (e p) -> d p e", e=2), 1.0 / EPS,
+                raw[:].rearrange("d (e p) -> d p e", e=2), MIN, MULT,
+            )
+
+        flipped_w = psum.tile([P, P], BF16, name="flipped_w", tag="flipped0")
         w_sumsq = held.tile([P, 1], F32, name="w_sumsq")
         w_inverse = held.tile([P, 1], F32, name="w_inverse")
         w_scale = held.tile([P, 1], F32, name="w_scale")
+        w_squares = held.tile([P, P], F32, name="w_squares")
         nc.tensor.transpose(flipped_w[:], weights[:], identity[:])
-        nc.scalar.activation(squares_s[:], flipped_w[:], SQUARE, accum_out=w_sumsq[:])
+        nc.scalar.activation(w_squares[:], flipped_w[:], SQUARE, accum_out=w_sumsq[:])
         nc.scalar.activation(w_inverse[:], w_sumsq[:], RSQRT, scale=TEMPERATURE * TEMPERATURE)
         nc.vector.tensor_scalar_min(w_scale[:], w_inverse[:], 1.0 / (TEMPERATURE * EPS))
 
         for j in range(2):
-            logits = psum.tile([P, PIECE], F32, name=f"logits{j}")
+            logits = psum.tile([P, PIECE], F32, name=f"logits{j}", tag=f"flipped{j + 1}")
             scaled = held.tile([P, PIECE], F32, name=f"scaled{j}")
             piece = offsets[:, j * (PIECE // 16) : (j + 1) * (PIECE // 16)]
             nc.tensor.matmul(logits[:], weights[:], window[:].indirect(piece), start=True, stop=True)

@@ -98,7 +98,10 @@ def tile_memcontrastiveloss_kernel(tc, table, w, offs, out):
             nc.tensor.matmul(logits[:], weights[:], window[:].indirect(piece), start=True, stop=True)
             if j == 0:
                 nc.vector.tensor_scalar_mul(scaled[:], logits[:], w_scale[:])
-                nc.sync.dma_start(out[:, j * PIECE : (j + 1) * PIECE], scaled[:])
             else:
                 nc.scalar.activation(scaled[:], logits[:], COPY, scale=w_scale[:])
-                nc.scalar.dma_start(out[:, j * PIECE : (j + 1) * PIECE], scaled[:])
+            for queue, first in ((nc.scalar, 0), (nc.sync, PIECE // 2)):
+                queue.dma_start(
+                    out[:, j * PIECE + first : j * PIECE + first + PIECE // 2],
+                    scaled[:, first : first + PIECE // 2],
+                )

@@ -74,7 +74,7 @@ def tile_memcontrastiveloss_kernel(tc, table, w, offs, out):
                     identity_f32[:],
                 )
             raw = held.tile([P, CHUNK], BF16, name=f"raw{c}")
-            nc.scalar.copy(raw[:], flipped[c][:])
+            nc.vector.tensor_copy(raw[:], flipped[c][:])
             nc.vector.scalar_tensor_tensor(
                 window[:, c * CHUNK : (c + 1) * CHUNK].rearrange("d (p e) -> d p e", e=2),
                 spread[:].rearrange("d (e p) -> d p e", e=2), 1.0 / EPS,

@@ -6,7 +6,9 @@ SLOTS = 1024
 PICKED = 512
 CHUNK = 2 * P
 CHUNKS = SLOTS // CHUNK
-PIECE = PICKED // 2
+PIECES = 4
+PIECE = PICKED // PIECES
+LOGITS_BANKS = ("flipped1", "flipped2", "flipped3", "spread0")
 PAD = 8
 TEMPERATURE = 0.07
 EPS = 1e-12
@@ -91,17 +93,15 @@ def tile_memcontrastiveloss_kernel(tc, table, w, offs, out):
         nc.scalar.activation(w_inverse[:], w_sumsq[:], RSQRT, scale=TEMPERATURE * TEMPERATURE)
         nc.vector.tensor_scalar_min(w_scale[:], w_inverse[:], 1.0 / (TEMPERATURE * EPS))
 
-        for j in range(2):
-            logits = psum.tile([P, PIECE], F32, name=f"logits{j}", tag=f"flipped{j + 1}")
+        for j in range(PIECES):
+            logits = psum.tile([P, PIECE], F32, name=f"logits{j}", tag=LOGITS_BANKS[j])
             scaled = held.tile([P, PIECE], F32, name=f"scaled{j}")
             piece = offsets[:, j * (PIECE // 16) : (j + 1) * (PIECE // 16)]
             nc.tensor.matmul(logits[:], weights[:], window[:].indirect(piece), start=True, stop=True)
-            if j == 0:
+            if j % 2 == 0:
                 nc.vector.tensor_scalar_mul(scaled[:], logits[:], w_scale[:])
+                queue = nc.sync
             else:
                 nc.scalar.activation(scaled[:], logits[:], COPY, scale=w_scale[:])
-            for queue, first in ((nc.scalar, 0), (nc.sync, PIECE // 2)):
-                queue.dma_start(
-                    out[:, j * PIECE + first : j * PIECE + first + PIECE // 2],
-                    scaled[:, first : first + PIECE // 2],
-                )
+                queue = nc.scalar
+            queue.dma_start(out[:, j * PIECE : (j + 1) * PIECE], scaled[:])

@@ -58,13 +58,16 @@ def tile_memcontrastiveloss_kernel(tc, table, w, offs, out):
                 )
             sumsq.append(held.tile([P, 2, PAD], F32, name=f"sumsq{c}"))
             squares = held.tile([P, 2, P], F32, name=f"squares{c}")
-            nc.scalar.activation(
-                squares[:, 0, :], rows[c][:, 0, :], SQUARE, accum_out=sumsq[c][:, 0, 0:1]
-            )
-            nc.vector.scalar_tensor_tensor(
-                squares[:, 1, :], rows[c][:, 1, :], 1.0, rows[c][:, 1, :], MULT, MULT,
-                accum_out=sumsq[c][:, 1, 0:1],
-            )
+            for e in range(2):
+                if e == 0 and c < CHUNKS // 2:
+                    nc.scalar.activation(
+                        squares[:, e, :], rows[c][:, e, :], SQUARE, accum_out=sumsq[c][:, e, 0:1]
+                    )
+                else:
+                    nc.vector.scalar_tensor_tensor(
+                        squares[:, e, :], rows[c][:, e, :], 1.0, rows[c][:, e, :], MULT, MULT,
+                        accum_out=sumsq[c][:, e, 0:1],
+                    )
 
         for c in range(CHUNKS):
             inverse = held.tile([P, 2, 1], F32, name=f"inverse{c}")

@@ -29,8 +29,7 @@ def tile_memcontrastiveloss_kernel(tc, table, w, offs, out):
         rows = []
         for c in range(CHUNKS):
             chunk = held.tile([P, 2, P], BF16, name=f"rows{c}")
-            queue = nc.sync if c % 2 == 0 else nc.scalar
-            queue.dma_start(
+            nc.sync.dma_start(
                 chunk[:], table[c * CHUNK : (c + 1) * CHUNK, :].rearrange("(p e) d -> p e d", e=2)
             )
             rows.append(chunk)

@@ -68,6 +68,16 @@ def tile_memcontrastiveloss_kernel(tc, table, w, offs, out):
                         accum_out=sumsq[c][:, e, 0:1],
                     )
 
+        flipped_w = psum.tile([P, P], BF16, name="flipped_w", tag="spread3")
+        w_sumsq = held.tile([P, 1], F32, name="w_sumsq")
+        w_inverse = held.tile([P, 1], F32, name="w_inverse")
+        w_scale = held.tile([P, 1], F32, name="w_scale")
+        w_squares = held.tile([P, P], F32, name="w_squares")
+        nc.tensor.transpose(flipped_w[:], weights[:], identity[:])
+        nc.scalar.activation(w_squares[:], flipped_w[:], SQUARE, accum_out=w_sumsq[:])
+        nc.scalar.activation(w_inverse[:], w_sumsq[:], RSQRT, scale=TEMPERATURE * TEMPERATURE)
+        nc.vector.tensor_scalar_min(w_scale[:], w_inverse[:], 1.0 / (TEMPERATURE * EPS))
+
         for c in range(CHUNKS):
             inverse = held.tile([P, 2, 1], F32, name=f"inverse{c}")
             nc.scalar.activation(inverse[:], sumsq[c][:, :, 0:1], RSQRT)
@@ -84,16 +94,6 @@ def tile_memcontrastiveloss_kernel(tc, table, w, offs, out):
                 spread[:].rearrange("d (e p) -> d p e", e=2), 1.0 / EPS,
                 raw[:].rearrange("d (e p) -> d p e", e=2), MIN, MULT,
             )
-
-        flipped_w = psum.tile([P, P], BF16, name="flipped_w", tag="flipped0")
-        w_sumsq = held.tile([P, 1], F32, name="w_sumsq")
-        w_inverse = held.tile([P, 1], F32, name="w_inverse")
-        w_scale = held.tile([P, 1], F32, name="w_scale")
-        w_squares = held.tile([P, P], F32, name="w_squares")
-        nc.tensor.transpose(flipped_w[:], weights[:], identity[:])
-        nc.scalar.activation(w_squares[:], flipped_w[:], SQUARE, accum_out=w_sumsq[:])
-        nc.scalar.activation(w_inverse[:], w_sumsq[:], RSQRT, scale=TEMPERATURE * TEMPERATURE)
-        nc.vector.tensor_scalar_min(w_scale[:], w_inverse[:], 1.0 / (TEMPERATURE * EPS))
 
         for j in range(PIECES):
             logits = psum.tile([P, PIECE], F32, name=f"logits{j}", tag=LOGITS_BANKS[j])

@@ -58,7 +58,7 @@ def tile_memcontrastiveloss_kernel(tc, table, w, offs, out):
             sumsq.append(held.tile([P, 2, PAD], F32, name=f"sumsq{c}"))
             squares = held.tile([P, 2, P], F32, name=f"squares{c}")
             for e in range(2):
-                if e == 0 and c < CHUNKS // 2:
+                if e == 0 and c != CHUNKS - 2:
                     nc.scalar.activation(
                         squares[:, e, :], rows[c][:, e, :], SQUARE, accum_out=sumsq[c][:, e, 0:1]
                     )
@@ -68,15 +68,17 @@ def tile_memcontrastiveloss_kernel(tc, table, w, offs, out):
                         accum_out=sumsq[c][:, e, 0:1],
                     )
 
-        flipped_w = psum.tile([P, P], BF16, name="flipped_w", tag="spread3")
-        w_sumsq = held.tile([P, 1], F32, name="w_sumsq")
-        w_inverse = held.tile([P, 1], F32, name="w_inverse")
         w_scale = held.tile([P, 1], F32, name="w_scale")
-        w_squares = held.tile([P, P], F32, name="w_squares")
-        nc.tensor.transpose(flipped_w[:], weights[:], identity[:])
-        nc.scalar.activation(w_squares[:], flipped_w[:], SQUARE, accum_out=w_sumsq[:])
-        nc.scalar.activation(w_inverse[:], w_sumsq[:], RSQRT, scale=TEMPERATURE * TEMPERATURE)
-        nc.vector.tensor_scalar_min(w_scale[:], w_inverse[:], 1.0 / (TEMPERATURE * EPS))
+
+        def scale_of_predictions():
+            flipped_w = psum.tile([P, P], BF16, name="flipped_w", tag="flipped0")
+            w_sumsq = held.tile([P, 1], F32, name="w_sumsq")
+            w_inverse = held.tile([P, 1], F32, name="w_inverse")
+            w_squares = held.tile([P, P], F32, name="w_squares")
+            nc.tensor.transpose(flipped_w[:], weights[:], identity[:])
+            nc.scalar.activation(w_squares[:], flipped_w[:], SQUARE, accum_out=w_sumsq[:])
+            nc.scalar.activation(w_inverse[:], w_sumsq[:], RSQRT, scale=TEMPERATURE * TEMPERATURE)
+            nc.vector.tensor_scalar_min(w_scale[:], w_inverse[:], 1.0 / (TEMPERATURE * EPS))
 
         for c in range(CHUNKS):
             inverse = held.tile([P, 2, 1], F32, name=f"inverse{c}")
@@ -94,6 +96,8 @@ def tile_memcontrastiveloss_kernel(tc, table, w, offs, out):
                 spread[:].rearrange("d (e p) -> d p e", e=2), 1.0 / EPS,
                 raw[:].rearrange("d (e p) -> d p e", e=2), MIN, MULT,
             )
+            if c == CHUNKS // 2 - 1:
+                scale_of_predictions()
 
         for j in range(PIECES):
             logits = psum.tile([P, PIECE], F32, name=f"logits{j}", tag=LOGITS_BANKS[j])

import concourse.mybir as mybir
from concourse.masks import make_identity

P = 128
SLOTS = 1024
PICKED = 512
CHUNK = 2 * P
CHUNKS = SLOTS // CHUNK
PIECES = 4
PIECE = PICKED // PIECES
LOGITS_BANKS = ("flipped1", "flipped2", "flipped3", "spread0")
PAD = 8
TEMPERATURE = 0.07
EPS = 1e-12
FLOPS = 2 * P * P * PICKED

BF16, F32, U16 = mybir.dt.bfloat16, mybir.dt.float32, mybir.dt.uint16
SQUARE = mybir.ActivationFunctionType.Square
RSQRT = mybir.ActivationFunctionType.Abs_reciprocal_sqrt
COPY = mybir.ActivationFunctionType.Copy
MULT, MIN = mybir.AluOpType.mult, mybir.AluOpType.min

def tile_memcontrastiveloss_kernel(tc, table, w, offs, out):
    nc = tc.nc
    with (
        tc.tile_pool(name="held", bufs=1) as held,
        tc.psum_pool(name="psum", bufs=1) as psum,
    ):
        rows = []
        for c in range(CHUNKS):
            chunk = held.tile([P, 2, P], BF16, name=f"rows{c}")
            nc.sync.dma_start(
                chunk[:], table[c * CHUNK : (c + 1) * CHUNK, :].rearrange("(p e) d -> p e d", e=2)
            )
            rows.append(chunk)
        offsets = held.tile([P, PICKED // 16], U16, name="offsets")
        nc.sync.dma_start(offsets[:], offs)
        weights = held.tile([P, P], BF16, name="weights")
        nc.sync.dma_start(weights[:], w)
        identity = held.tile([P, P], BF16, name="identity")
        make_identity(nc, identity[:])
        identity_f32 = held.tile([P, P], F32, name="identity_f32")
        make_identity(nc, identity_f32[:])

        scratch = held.tile([P, 1], F32, name="scratch")
        nc.vector.memset(scratch[:], 1.0)
        nc.scalar.activation(scratch[:], scratch[:], RSQRT)

        window = held.tile([P, SLOTS], BF16, name="window")

        flipped, sumsq = [], []
        for c in range(CHUNKS):
            flipped.append(psum.tile([P, CHUNK], BF16, name=f"flipped{c}"))
            for e in range(2):
                nc.tensor.transpose(
                    flipped[c][:, e * P : (e + 1) * P], rows[c][:, e, :], identity[:]
                )
            sumsq.append(held.tile([P, 2, PAD], F32, name=f"sumsq{c}"))
            squares = held.tile([P, 2, P], F32, name=f"squares{c}")
            for e in range(2):
                if e == 0 and c != CHUNKS - 2:
                    nc.scalar.activation(
                        squares[:, e, :], rows[c][:, e, :], SQUARE, accum_out=sumsq[c][:, e, 0:1]
                    )
                else:
                    nc.vector.scalar_tensor_tensor(
                        squares[:, e, :], rows[c][:, e, :], 1.0, rows[c][:, e, :], MULT, MULT,
                        accum_out=sumsq[c][:, e, 0:1],
                    )

        w_scale = held.tile([P, 1], F32, name="w_scale")

        def scale_of_predictions():
            flipped_w = psum.tile([P, P], BF16, name="flipped_w", tag="flipped0")
            w_sumsq = held.tile([P, 1], F32, name="w_sumsq")
            w_inverse = held.tile([P, 1], F32, name="w_inverse")
            w_squares = held.tile([P, P], F32, name="w_squares")
            nc.tensor.transpose(flipped_w[:], weights[:], identity[:])
            nc.scalar.activation(w_squares[:], flipped_w[:], SQUARE, accum_out=w_sumsq[:])
            nc.scalar.activation(w_inverse[:], w_sumsq[:], RSQRT, scale=TEMPERATURE * TEMPERATURE)
            nc.vector.tensor_scalar_min(w_scale[:], w_inverse[:], 1.0 / (TEMPERATURE * EPS))

        for c in range(CHUNKS):
            inverse = held.tile([P, 2, 1], F32, name=f"inverse{c}")
            nc.scalar.activation(inverse[:], sumsq[c][:, :, 0:1], RSQRT)
            spread = psum.tile([P, CHUNK], F32, name=f"spread{c}")
            for e in range(2):
                nc.tensor.transpose(
                    spread[:, e * P : (e + 1) * P], inverse[:, e, :].to_broadcast([P, P]),
                    identity_f32[:],
                )
            raw = held.tile([P, CHUNK], BF16, name=f"raw{c}")
            nc.vector.tensor_copy(raw[:], flipped[c][:])
            nc.vector.scalar_tensor_tensor(
                window[:, c * CHUNK : (c + 1) * CHUNK].rearrange("d (p e) -> d p e", e=2),
                spread[:].rearrange("d (e p) -> d p e", e=2), 1.0 / EPS,
                raw[:].rearrange("d (e p) -> d p e", e=2), MIN, MULT,
            )
            if c == CHUNKS // 2 - 1:
                scale_of_predictions()

        for j in range(PIECES):
            logits = psum.tile([P, PIECE], F32, name=f"logits{j}", tag=LOGITS_BANKS[j])
            scaled = held.tile([P, PIECE], F32, name=f"scaled{j}")
            piece = offsets[:, j * (PIECE // 16) : (j + 1) * (PIECE // 16)]
            nc.tensor.matmul(logits[:], weights[:], window[:].indirect(piece), start=True, stop=True)
            if j % 2 == 0:
                nc.vector.tensor_scalar_mul(scaled[:], logits[:], w_scale[:])
                queue = nc.sync
            else:
                nc.scalar.activation(scaled[:], logits[:], COPY, scale=w_scale[:])
                queue = nc.scalar
            queue.dma_start(out[:, j * PIECE : (j + 1) * PIECE], scaled[:])
